import numpy as np
import ml_dtypes


def mxq(x, axis, fmt="e4m3"):
    dtype, down = {"e4m3": (ml_dtypes.float8_e4m3fn, 7), "e5m2": (ml_dtypes.float8_e5m2, 14)}[fmt]
    v = np.moveaxis(np.asarray(x, np.float32).astype(ml_dtypes.bfloat16).astype(np.float64), axis, -1)
    blocks = v.reshape(v.shape[:-1] + (-1, 32))
    amax = np.abs(blocks).max(-1, keepdims=True)
    byte = np.maximum(np.where(amax > 0, np.frexp(amax)[1] - 1 + 127, 0) - down, 1)
    scale = np.exp2(byte - 127.0)
    codes = (blocks / scale).astype(np.float32).astype(dtype).astype(np.float64)
    return np.moveaxis((codes * scale).reshape(v.shape), -1, axis)


WIDE = False


def mx_kscale(k):
    if not WIDE:
        return np.ones(k)
    levels = np.array([10, -10, 5, -5, 0])
    a = np.random.permutation(np.resize(levels, k // 512 * 4)).reshape(k // 512, 4)
    idx = np.arange(k)
    return np.exp2(a[idx // 512, idx % 128 // 32])


BF16 = ml_dtypes.bfloat16


def bf(x):
    return np.asarray(x, np.float32).astype(BF16)


def f64(x):
    return np.asarray(x).astype(np.float64)


E2M1 = np.array([0.0, 0.5, 1.0, 1.5, 2.0, 3.0, 4.0, 6.0, -0.0, -0.5, -1.0, -1.5, -2.0, -3.0, -4.0, -6.0])


def pack_weight(w, fmt):
    k, n = w.shape
    w = f64(bf(w)).reshape(k // 32, 32, n)
    amax = np.abs(w).max(1)
    if fmt == "e4m3":
        byte = np.frexp(amax)[1] - 1 + 127 - 7
    else:
        mant, ex = np.frexp(amax / 6.0)
        byte = np.where(mant > 0.5, ex, ex - 1) + 127
    byte = np.clip(np.where(amax > 0, byte, 1), 1, 254)
    scaled = (w * np.exp2(127.0 - byte)[:, None, :]).reshape(k, n).astype(np.float32)
    by_word = np.ascontiguousarray(scaled.reshape(k // 512, 128, 4, n).transpose(0, 1, 3, 2))
    if fmt == "e4m3":
        words = by_word.astype(ml_dtypes.float8_e4m3fn).view(np.uint8)
    else:
        c = by_word.astype(ml_dtypes.float4_e2m1fn).view(np.uint8) & 0xF
        words = c[..., 0::2] | (c[..., 1::2] << 4)
    return np.ascontiguousarray(words), np.ascontiguousarray(byte.astype(np.uint8).reshape(k // 512, 16, n))


def unpack_weight(words, scales, fmt):
    g, p, n, _ = words.shape
    if fmt == "e4m3":
        vals = np.ascontiguousarray(words).view(ml_dtypes.float8_e4m3fn).astype(np.float64)
    else:
        nib = np.empty((g, p, n, 4), np.uint8)
        nib[..., 0::2] = words & 0xF
        nib[..., 1::2] = words >> 4
        vals = E2M1[nib]
    vals = vals * np.repeat(np.exp2(scales.astype(np.float64) - 127.0), 8, axis=1)[..., None]
    return vals.transpose(0, 1, 3, 2).reshape(g * 512, n)


N, D, C, M = 12288, 512, 16, 16


def setup_inputs():
    s = mx_kscale(D)
    x = bf(np.random.standard_normal((N, D)) * s)
    x_var = bf(0.1 + 4.0 * np.random.standard_normal((N, D)) ** 2)
    stack = (np.random.standard_normal((C, M, D)) * 0.5 / np.sqrt(D) / s).swapaxes(1, 2)
    words, scales = pack_weight(stack.reshape(-1, M), "e4m3")
    proto_var = bf(0.1 + 4.0 * np.random.standard_normal((C, M, D)) ** 2)
    return {"x": x,
            "x_var": x_var,
            "prototypes_words": words,
            "prototypes_scales": scales,
            "proto_var": proto_var}


def reference(x, x_var, prototypes_words, prototypes_scales, proto_var):
    x, x_var, proto_var = f64(x), f64(x_var), f64(proto_var)
    lamda = 1.0 / x.shape[-1]
    dot = (mxq(x, 1, "e4m3") @ unpack_weight(prototypes_words, prototypes_scales, "e4m3").reshape(C, D, M).swapaxes(1, 2).reshape(C * M, D).T).reshape(N, C, M)
    cross = (mxq(np.sqrt(x_var), 1, "e4m3") @ mxq(np.sqrt(proto_var).reshape(C * M, D), 1, "e4m3").T).reshape(N, C, M)
    w2 = (2.0 - 2.0 * dot
          + lamda * (np.sum(x_var, axis=-1)[:, None, None]
                     + np.sum(proto_var, axis=-1)[None, :, :]
                     - 2.0 * cross))
    return -w2

@@ -1,0 +1,210 @@
+from contextlib import ExitStack
+
+import concourse.mybir as mybir
+from concourse.masks import make_identity
+
+F32 = mybir.dt.float32
+BF16 = mybir.dt.bfloat16
+I32 = mybir.dt.int32
+U32 = mybir.dt.uint32
+U8 = mybir.dt.uint8
+FP8X4 = mybir.dt.float8_e4m3fn_x4
+ALU = mybir.AluOpType
+ACT = mybir.ActivationFunctionType
+
+P = 128
+ROWS = 12288
+D = 512
+PER_CLASS = 16
+PROTOS = 256
+LAMDA = 1.0 / D
+PACK = 4
+GROUP_TILES = 8
+PAIR = 2
+GROUPS = ROWS // (P * GROUP_TILES)
+
+FLOPS = 2 * 2 * ROWS * D * PROTOS
+
+
+def tile_probprotoseghead_t_e_kernel(
+    tc, x, x_var, prototypes_words, prototypes_scales, proto_var, out
+):
+    nc = tc.nc
+    x_groups = x.rearrange("(g p t) d -> g p t d", p=P, t=GROUP_TILES)
+    var_groups = x_var.rearrange("(g p t) d -> g p t d", p=P, t=GROUP_TILES)
+    out_groups = out.rearrange("(g p t) c m -> g p t (c m)", p=P, t=GROUP_TILES)
+
+    with ExitStack() as stack:
+        const = stack.enter_context(tc.tile_pool(name="const", bufs=1))
+        rows = stack.enter_context(tc.tile_pool(name="rows", bufs=3))
+        work = stack.enter_context(tc.tile_pool(name="work", bufs=3))
+        setup_psum = stack.enter_context(tc.psum_pool(name="setup_psum", bufs=1))
+        psum = stack.enter_context(tc.psum_pool(name="psum", bufs=2))
+
+        ident = const.tile([P, P], F32)
+        make_identity(nc, ident[:])
+
+        pv = const.tile([P, 2, D], BF16)
+        nc.sync.dma_start(
+            out=pv[:],
+            in_=proto_var.rearrange("c m d -> (c m) d").rearrange("(h p) d -> p h d", p=P),
+        )
+
+        proto_codes = const.tile([P, PROTOS], U32, align_bytes=64)
+        nc.sync.dma_start(
+            out=proto_codes[:].bitcast(I32).rearrange("p (c m) -> p c m", m=PER_CLASS),
+            in_=prototypes_words.rearrange("c p m t -> c p (m t)")
+            .bitcast(I32)
+            .rearrange("c p m -> p c m"),
+        )
+        proto_scales = const.tile([P, PROTOS], U8, align_bytes=64)
+        nc.vector.memset(proto_scales[:].bitcast(I32), 0)
+        scale_words = prototypes_scales.bitcast(I32)
+        for quadrant in range(4):
+            nc.sync.dma_start(
+                out=proto_scales[32 * quadrant : 32 * quadrant + 4, :]
+                .bitcast(I32)
+                .rearrange("r (c w) -> r c w", w=PER_CLASS // 4),
+                in_=scale_words[:, 4 * quadrant : 4 * quadrant + 4, :].rearrange("c r w -> r c w"),
+            )
+
+        pv_sum = const.tile([P, 2], F32)
+        nc.vector.tensor_reduce(out=pv_sum[:], in_=pv[:], axis=mybir.AxisListType.X, op=ALU.add)
+        pv_term = const.tile([P, 2], F32)
+        nc.vector.tensor_scalar(
+            out=pv_term[:], in0=pv_sum[:], scalar1=-LAMDA, scalar2=-2.0, op0=ALU.mult, op1=ALU.add
+        )
+        spread = setup_psum.tile([P, 2, P], F32)
+        for h in range(2):
+            nc.tensor.transpose(
+                out=spread[:, h, :],
+                in_=pv_term[:, h : h + 1].to_broadcast([P, P]),
+                identity=ident[:],
+            )
+        proto_term = const.tile([P, PROTOS], F32)
+        nc.vector.tensor_copy(out=proto_term[:], in_=spread[:].rearrange("p h c -> p (h c)"))
+
+        pv_t = setup_psum.tile([P, 2, 2, P], F32)
+        for h in range(2):
+            for u in range(2):
+                nc.tensor.transpose(
+                    out=pv_t[:, h, u, :],
+                    in_=pv[:, h, :].bitcast(F32)[:, u * P : (u + 1) * P],
+                    identity=ident[:],
+                )
+        pv_root = const.tile([P, 2, P, PACK], F32)
+        for h in range(2):
+            nc.scalar.activation(
+                out=pv_root[:, h].rearrange("p c (u e) -> p c u e", e=2),
+                in_=pv_t[:, h].bitcast(BF16).rearrange("p u (c e) -> p c u e", e=2),
+                func=ACT.Sqrt,
+            )
+        pv_grouped = const.tile([P, PROTOS * PACK], BF16, align_bytes=64)
+        nc.vector.tensor_scalar(
+            out=pv_grouped[:],
+            in0=pv_root[:].rearrange("p h c t -> p (h c t)"),
+            scalar1=LAMDA,
+            scalar2=None,
+            op0=ALU.mult,
+        )
+        root_codes = const.tile([P, PROTOS], U32, align_bytes=64)
+        root_scales = const.tile([P, PROTOS], U8, align_bytes=64)
+        nc.vector.quantize_mx(
+            out=root_codes[:].bitcast(FP8X4), scales=root_scales[:], in_=pv_grouped[:]
+        )
+
+        for g in range(GROUPS):
+            x_rows = rows.tile([P, GROUP_TILES, D], BF16)
+            nc.sync.dma_start(out=x_rows[:], in_=x_groups[g])
+            var_rows = rows.tile([P, GROUP_TILES, D], BF16)
+            nc.sync.dma_start(out=var_rows[:], in_=var_groups[g])
+            out_rows = rows.tile([P, GROUP_TILES, PROTOS], F32)
+
+            var_term = work.tile([P, GROUP_TILES], F32)
+            for t in range(GROUP_TILES):
+                scaled = work.tile([P, D], BF16)
+                nc.vector.tensor_scalar(
+                    out=scaled[:],
+                    in0=var_rows[:, t, :],
+                    scalar1=-LAMDA,
+                    scalar2=None,
+                    op0=ALU.mult,
+                    op1=ALU.add,
+                    accum_out=var_term[:, t : t + 1],
+                )
+
+            for first in range(0, GROUP_TILES, PAIR):
+                x_t = psum.tile([P, PAIR, 2, P], F32)
+                var_t = psum.tile([P, PAIR, 2, P], F32)
+                for i in range(PAIR):
+                    for u in range(2):
+                        nc.tensor.transpose(
+                            out=x_t[:, i, u, :],
+                            in_=x_rows[:, first + i, :].bitcast(F32)[:, u : D // 2 : 2],
+                            identity=ident[:],
+                        )
+                for i in range(PAIR):
+                    for u in range(2):
+                        nc.tensor.transpose(
+                            out=var_t[:, i, u, :],
+                            in_=var_rows[:, first + i, :].bitcast(F32)[:, u * P : (u + 1) * P],
+                            identity=ident[:],
+                        )
+
+                grouped = work.tile([P, 2, PAIR, P, PACK], BF16, align_bytes=64)
+                nc.scalar.copy(
+                    out=grouped[:, 0].bitcast(F32), in_=x_t[:].rearrange("p i u n -> p i n u")
+                )
+                for i in range(PAIR):
+                    nc.scalar.activation(
+                        out=grouped[:, 1, i].rearrange("p n (u e) -> p n u e", e=2),
+                        in_=var_t[:, i].bitcast(BF16).rearrange("p u (n e) -> p n u e", e=2),
+                        func=ACT.Sqrt,
+                    )
+                codes = work.tile([P, 2 * PAIR * P], U32, align_bytes=64)
+                scales = work.tile([P, 2 * PAIR * P], U8, align_bytes=64)
+                nc.vector.quantize_mx(
+                    out=codes[:].bitcast(FP8X4),
+                    scales=scales[:],
+                    in_=grouped[:].rearrange("p k i n t -> p (k i n t)"),
+                )
+
+                acc = psum.tile([P, PAIR, PROTOS], F32)
+                bias = work.tile([P, PAIR, PROTOS], F32)
+                for i in range(PAIR):
+                    x_cols = slice(i * P, (i + 1) * P)
+                    root_cols = slice((PAIR + i) * P, (PAIR + i + 1) * P)
+                    nc.tensor.matmul_mx(
+                        out=acc[:, i, :],
+                        lhsT=codes[:, x_cols].bitcast(FP8X4),
+                        lhsT_scale=scales[:, x_cols],
+                        rhs=proto_codes[:].bitcast(FP8X4),
+                        rhs_scale=proto_scales[:],
+                        start=True,
+                        stop=False,
+                    )
+                    nc.tensor.matmul_mx(
+                        out=acc[:, i, :],
+                        lhsT=codes[:, root_cols].bitcast(FP8X4),
+                        lhsT_scale=scales[:, root_cols],
+                        rhs=root_codes[:].bitcast(FP8X4),
+                        rhs_scale=root_scales[:],
+                        start=False,
+                        stop=True,
+                    )
+                    nc.vector.tensor_scalar(
+                        out=bias[:, i, :],
+                        in0=proto_term[:],
+                        scalar1=var_term[:, first + i : first + i + 1],
+                        scalar2=None,
+                        op0=ALU.add,
+                    )
+                nc.vector.scalar_tensor_tensor(
+                    out=out_rows[:, first : first + PAIR, :],
+                    in0=acc[:],
+                    scalar=2.0,
+                    in1=bias[:],
+                    op0=ALU.mult,
+                    op1=ALU.add,
+                )
+            nc.sync.dma_start(out=out_groups[g], in_=out_rows[:])

@@ -19,9 +19,12 @@ PER_CLASS = 16
 PROTOS = 256
 LAMDA = 1.0 / D
 PACK = 4
-GROUP_TILES = 8
 PAIR = 2
+GROUP_TILES = 4
+GROUP_UNITS = GROUP_TILES // PAIR
 GROUPS = ROWS // (P * GROUP_TILES)
+UNITS = GROUPS * GROUP_UNITS
+LOADS_AHEAD = 5
 
 FLOPS = 2 * 2 * ROWS * D * PROTOS
 
@@ -36,8 +39,9 @@ def tile_probprotoseghead_t_e_kernel(
 
     with ExitStack() as stack:
         const = stack.enter_context(tc.tile_pool(name="const", bufs=1))
-        rows = stack.enter_context(tc.tile_pool(name="rows", bufs=3))
-        work = stack.enter_context(tc.tile_pool(name="work", bufs=3))
+        rows = stack.enter_context(tc.tile_pool(name="rows", bufs=LOADS_AHEAD + 1))
+        results = stack.enter_context(tc.tile_pool(name="results", bufs=3))
+        work = stack.enter_context(tc.tile_pool(name="work", bufs=4))
         setup_psum = stack.enter_context(tc.psum_pool(name="setup_psum", bufs=1))
         psum = stack.enter_context(tc.psum_pool(name="psum", bufs=2))
 
@@ -113,98 +117,153 @@ def tile_probprotoseghead_t_e_kernel(
             out=root_codes[:].bitcast(FP8X4), scales=root_scales[:], in_=pv_grouped[:]
         )
 
-        for g in range(GROUPS):
-            x_rows = rows.tile([P, GROUP_TILES, D], BF16)
-            nc.sync.dma_start(out=x_rows[:], in_=x_groups[g])
-            var_rows = rows.tile([P, GROUP_TILES, D], BF16)
-            nc.sync.dma_start(out=var_rows[:], in_=var_groups[g])
-            out_rows = rows.tile([P, GROUP_TILES, PROTOS], F32)
+        x_rows = {}
+        var_rows = {}
+        out_rows = {}
+        var_term = {}
+        bias = {}
+        x_t = {}
+        var_t = {}
+        grouped = {}
+        codes = {}
+        scales = {}
+        acc = {}
 
-            var_term = work.tile([P, GROUP_TILES], F32)
-            for t in range(GROUP_TILES):
+        def load(g):
+            x_tile = rows.tile([P, GROUP_TILES, D], BF16)
+            nc.sync.dma_start(out=x_tile[:], in_=x_groups[g])
+            var_tile = rows.tile([P, GROUP_TILES, D], BF16)
+            nc.sync.dma_start(out=var_tile[:], in_=var_groups[g])
+            x_rows[g] = x_tile
+            var_rows[g] = var_tile
+
+        def sums(s):
+            g, first = s // GROUP_UNITS, PAIR * (s % GROUP_UNITS)
+            term_tile = work.tile([P, PAIR], F32)
+            bias_tile = work.tile([P, PAIR, PROTOS], F32)
+            for i in range(PAIR):
                 scaled = work.tile([P, D], BF16)
                 nc.vector.tensor_scalar(
                     out=scaled[:],
-                    in0=var_rows[:, t, :],
+                    in0=var_rows[g][:, first + i, :],
                     scalar1=-LAMDA,
                     scalar2=None,
                     op0=ALU.mult,
                     op1=ALU.add,
-                    accum_out=var_term[:, t : t + 1],
+                    accum_out=term_tile[:, i : i + 1],
                 )
+            for i in range(PAIR):
+                nc.vector.tensor_scalar(
+                    out=bias_tile[:, i, :],
+                    in0=proto_term[:],
+                    scalar1=term_tile[:, i : i + 1],
+                    scalar2=1.0,
+                    op0=ALU.add,
+                    op1=ALU.mult,
+                )
+            var_term[s] = term_tile
+            bias[s] = bias_tile
 
-            for first in range(0, GROUP_TILES, PAIR):
-                x_t = psum.tile([P, PAIR, 2, P], F32)
-                var_t = psum.tile([P, PAIR, 2, P], F32)
-                for i in range(PAIR):
-                    for u in range(2):
-                        nc.tensor.transpose(
-                            out=x_t[:, i, u, :],
-                            in_=x_rows[:, first + i, :].bitcast(F32)[:, u : D // 2 : 2],
-                            identity=ident[:],
-                        )
-                for i in range(PAIR):
-                    for u in range(2):
-                        nc.tensor.transpose(
-                            out=var_t[:, i, u, :],
-                            in_=var_rows[:, first + i, :].bitcast(F32)[:, u * P : (u + 1) * P],
-                            identity=ident[:],
-                        )
+        def transposes(s):
+            g, first = s // GROUP_UNITS, PAIR * (s % GROUP_UNITS)
+            x_bank = psum.tile([P, PAIR, 2, P], F32)
+            var_bank = psum.tile([P, PAIR, 2, P], F32)
+            for i in range(PAIR):
+                for u in range(2):
+                    nc.tensor.transpose(
+                        out=x_bank[:, i, u, :],
+                        in_=x_rows[g][:, first + i, :].bitcast(F32)[:, u : D // 2 : 2],
+                        identity=ident[:],
+                    )
+            for i in range(PAIR):
+                for u in range(2):
+                    nc.tensor.transpose(
+                        out=var_bank[:, i, u, :],
+                        in_=var_rows[g][:, first + i, :].bitcast(F32)[:, u * P : (u + 1) * P],
+                        identity=ident[:],
+                    )
+            x_t[s] = x_bank
+            var_t[s] = var_bank
 
-                grouped = work.tile([P, 2, PAIR, P, PACK], BF16, align_bytes=64)
-                nc.scalar.copy(
-                    out=grouped[:, 0].bitcast(F32), in_=x_t[:].rearrange("p i u n -> p i n u")
+        def evacuate(s):
+            grouped_tile = work.tile([P, 2, PAIR, P, PACK], BF16, align_bytes=64)
+            nc.scalar.copy(
+                out=grouped_tile[:, 0].bitcast(F32), in_=x_t[s][:].rearrange("p i u n -> p i n u")
+            )
+            for i in range(PAIR):
+                nc.scalar.activation(
+                    out=grouped_tile[:, 1, i].rearrange("p n (u e) -> p n u e", e=2),
+                    in_=var_t[s][:, i].bitcast(BF16).rearrange("p u (n e) -> p n u e", e=2),
+                    func=ACT.Sqrt,
                 )
-                for i in range(PAIR):
-                    nc.scalar.activation(
-                        out=grouped[:, 1, i].rearrange("p n (u e) -> p n u e", e=2),
-                        in_=var_t[:, i].bitcast(BF16).rearrange("p u (n e) -> p n u e", e=2),
-                        func=ACT.Sqrt,
-                    )
-                codes = work.tile([P, 2 * PAIR * P], U32, align_bytes=64)
-                scales = work.tile([P, 2 * PAIR * P], U8, align_bytes=64)
-                nc.vector.quantize_mx(
-                    out=codes[:].bitcast(FP8X4),
-                    scales=scales[:],
-                    in_=grouped[:].rearrange("p k i n t -> p (k i n t)"),
-                )
+            grouped[s] = grouped_tile
 
-                acc = psum.tile([P, PAIR, PROTOS], F32)
-                bias = work.tile([P, PAIR, PROTOS], F32)
-                for i in range(PAIR):
-                    x_cols = slice(i * P, (i + 1) * P)
-                    root_cols = slice((PAIR + i) * P, (PAIR + i + 1) * P)
-                    nc.tensor.matmul_mx(
-                        out=acc[:, i, :],
-                        lhsT=codes[:, x_cols].bitcast(FP8X4),
-                        lhsT_scale=scales[:, x_cols],
-                        rhs=proto_codes[:].bitcast(FP8X4),
-                        rhs_scale=proto_scales[:],
-                        start=True,
-                        stop=False,
-                    )
-                    nc.tensor.matmul_mx(
-                        out=acc[:, i, :],
-                        lhsT=codes[:, root_cols].bitcast(FP8X4),
-                        lhsT_scale=scales[:, root_cols],
-                        rhs=root_codes[:].bitcast(FP8X4),
-                        rhs_scale=root_scales[:],
-                        start=False,
-                        stop=True,
-                    )
-                    nc.vector.tensor_scalar(
-                        out=bias[:, i, :],
-                        in0=proto_term[:],
-                        scalar1=var_term[:, first + i : first + i + 1],
-                        scalar2=None,
-                        op0=ALU.add,
-                    )
-                nc.vector.scalar_tensor_tensor(
-                    out=out_rows[:, first : first + PAIR, :],
-                    in0=acc[:],
-                    scalar=2.0,
-                    in1=bias[:],
-                    op0=ALU.mult,
-                    op1=ALU.add,
+        def quantise(s):
+            codes_tile = work.tile([P, 2 * PAIR * P], U32, align_bytes=64)
+            scales_tile = work.tile([P, 2 * PAIR * P], U8, align_bytes=64)
+            nc.vector.quantize_mx(
+                out=codes_tile[:].bitcast(FP8X4),
+                scales=scales_tile[:],
+                in_=grouped[s][:].rearrange("p k i n t -> p (k i n t)"),
+            )
+            codes[s] = codes_tile
+            scales[s] = scales_tile
+
+        def multiply(s):
+            acc_bank = psum.tile([P, PAIR, PROTOS], F32)
+            for i in range(PAIR):
+                x_cols = slice(i * P, (i + 1) * P)
+                root_cols = slice((PAIR + i) * P, (PAIR + i + 1) * P)
+                nc.tensor.matmul_mx(
+                    out=acc_bank[:, i, :],
+                    lhsT=codes[s][:, x_cols].bitcast(FP8X4),
+                    lhsT_scale=scales[s][:, x_cols],
+                    rhs=proto_codes[:].bitcast(FP8X4),
+                    rhs_scale=proto_scales[:],
+                    start=True,
+                    stop=False,
                 )
-            nc.sync.dma_start(out=out_groups[g], in_=out_rows[:])
+                nc.tensor.matmul_mx(
+                    out=acc_bank[:, i, :],
+                    lhsT=codes[s][:, root_cols].bitcast(FP8X4),
+                    lhsT_scale=scales[s][:, root_cols],
+                    rhs=root_codes[:].bitcast(FP8X4),
+                    rhs_scale=root_scales[:],
+                    start=False,
+                    stop=True,
+                )
+            acc[s] = acc_bank
+
+        def finish(s):
+            g, first = s // GROUP_UNITS, PAIR * (s % GROUP_UNITS)
+            if first == 0:
+                out_tile = results.tile([P, GROUP_TILES, PROTOS], F32)
+                out_rows[g] = out_tile
+            nc.vector.scalar_tensor_tensor(
+                out=out_rows[g][:, first : first + PAIR, :],
+                in0=acc[s][:],
+                scalar=2.0,
+                in1=bias[s][:],
+                op0=ALU.mult,
+                op1=ALU.add,
+            )
+            if first + PAIR == GROUP_TILES:
+                nc.sync.dma_start(out=out_groups[g], in_=out_rows[g][:])
+
+        with tc.manual_schedule():
+            for g in range(LOADS_AHEAD):
+                load(g)
+            for step in range(UNITS + 2):
+                if step < UNITS:
+                    if step % GROUP_UNITS == 0 and step // GROUP_UNITS + LOADS_AHEAD < GROUPS:
+                        load(step // GROUP_UNITS + LOADS_AHEAD)
+                    transposes(step)
+                    evacuate(step)
+                if step >= 2:
+                    multiply(step - 2)
+                if 1 <= step <= UNITS:
+                    quantise(step - 1)
+                if step >= 2:
+                    finish(step - 2)
+                if step < UNITS:
+                    sums(step)

@@ -153,7 +153,7 @@ def tile_probprotoseghead_t_e_kernel(
                     accum_out=term_tile[:, i : i + 1],
                 )
             for i in range(PAIR):
-                nc.vector.tensor_scalar(
+                nc.gpsimd.tensor_scalar(
                     out=bias_tile[:, i, :],
                     in0=proto_term[:],
                     scalar1=term_tile[:, i : i + 1],

@@ -107,7 +107,7 @@ def tile_probprotoseghead_t_e_kernel(
         nc.vector.tensor_scalar(
             out=pv_grouped[:],
             in0=pv_root[:].rearrange("p h c t -> p (h c t)"),
-            scalar1=LAMDA,
+            scalar1=2.0 * LAMDA,
             scalar2=None,
             op0=ALU.mult,
         )
@@ -214,15 +214,16 @@ def tile_probprotoseghead_t_e_kernel(
             for i in range(PAIR):
                 x_cols = slice(i * P, (i + 1) * P)
                 root_cols = slice((PAIR + i) * P, (PAIR + i + 1) * P)
-                nc.tensor.matmul_mx(
-                    out=acc_bank[:, i, :],
-                    lhsT=codes[s][:, x_cols].bitcast(FP8X4),
-                    lhsT_scale=scales[s][:, x_cols],
-                    rhs=proto_codes[:].bitcast(FP8X4),
-                    rhs_scale=proto_scales[:],
-                    start=True,
-                    stop=False,
-                )
+                for repeat in range(2):
+                    nc.tensor.matmul_mx(
+                        out=acc_bank[:, i, :],
+                        lhsT=codes[s][:, x_cols].bitcast(FP8X4),
+                        lhsT_scale=scales[s][:, x_cols],
+                        rhs=proto_codes[:].bitcast(FP8X4),
+                        rhs_scale=proto_scales[:],
+                        start=(repeat == 0),
+                        stop=False,
+                    )
                 nc.tensor.matmul_mx(
                     out=acc_bank[:, i, :],
                     lhsT=codes[s][:, root_cols].bitcast(FP8X4),
@@ -242,7 +243,7 @@ def tile_probprotoseghead_t_e_kernel(
             nc.vector.scalar_tensor_tensor(
                 out=out_rows[g][:, first : first + PAIR, :],
                 in0=acc[s][:],
-                scalar=2.0,
+                scalar=1.0,
                 in1=bias[s][:],
                 op0=ALU.mult,
                 op1=ALU.add,

@@ -121,7 +121,6 @@ def tile_probprotoseghead_t_e_kernel(
         var_rows = {}
         out_rows = {}
         var_term = {}
-        bias = {}
         x_t = {}
         var_t = {}
         grouped = {}
@@ -140,7 +139,6 @@ def tile_probprotoseghead_t_e_kernel(
         def sums(s):
             g, first = s // GROUP_UNITS, PAIR * (s % GROUP_UNITS)
             term_tile = work.tile([P, PAIR], F32)
-            bias_tile = work.tile([P, PAIR, PROTOS], F32)
             for i in range(PAIR):
                 scaled = work.tile([P, D], BF16)
                 nc.vector.tensor_scalar(
@@ -152,17 +150,7 @@ def tile_probprotoseghead_t_e_kernel(
                     op1=ALU.add,
                     accum_out=term_tile[:, i : i + 1],
                 )
-            for i in range(PAIR):
-                nc.gpsimd.tensor_scalar(
-                    out=bias_tile[:, i, :],
-                    in0=proto_term[:],
-                    scalar1=term_tile[:, i : i + 1],
-                    scalar2=1.0,
-                    op0=ALU.add,
-                    op1=ALU.mult,
-                )
             var_term[s] = term_tile
-            bias[s] = bias_tile
 
         def transposes(s):
             g, first = s // GROUP_UNITS, PAIR * (s % GROUP_UNITS)
@@ -240,14 +228,15 @@ def tile_probprotoseghead_t_e_kernel(
             if first == 0:
                 out_tile = results.tile([P, GROUP_TILES, PROTOS], F32)
                 out_rows[g] = out_tile
-            nc.vector.scalar_tensor_tensor(
-                out=out_rows[g][:, first : first + PAIR, :],
-                in0=acc[s][:],
-                scalar=1.0,
-                in1=bias[s][:],
-                op0=ALU.mult,
-                op1=ALU.add,
-            )
+            for i in range(PAIR):
+                nc.vector.scalar_tensor_tensor(
+                    out=out_rows[g][:, first + i, :],
+                    in0=acc[s][:, i, :],
+                    scalar=var_term[s][:, i : i + 1],
+                    in1=proto_term[:],
+                    op0=ALU.add,
+                    op1=ALU.add,
+                )
             if first + PAIR == GROUP_TILES:
                 nc.sync.dma_start(out=out_groups[g], in_=out_rows[g][:])
 

@@ -25,6 +25,7 @@ GROUP_UNITS = GROUP_TILES // PAIR
 GROUPS = ROWS // (P * GROUP_TILES)
 UNITS = GROUPS * GROUP_UNITS
 LOADS_AHEAD = 5
+SCALAR_SUM_EVERY = 6
 
 FLOPS = 2 * 2 * ROWS * D * PROTOS
 
@@ -42,6 +43,7 @@ def tile_probprotoseghead_t_e_kernel(
         rows = stack.enter_context(tc.tile_pool(name="rows", bufs=LOADS_AHEAD + 1))
         results = stack.enter_context(tc.tile_pool(name="results", bufs=3))
         work = stack.enter_context(tc.tile_pool(name="work", bufs=4))
+        terms = stack.enter_context(tc.tile_pool(name="terms", bufs=4 * PAIR))
         setup_psum = stack.enter_context(tc.psum_pool(name="setup_psum", bufs=1))
         psum = stack.enter_context(tc.psum_pool(name="psum", bufs=2))
 
@@ -138,19 +140,30 @@ def tile_probprotoseghead_t_e_kernel(
 
         def sums(s):
             g, first = s // GROUP_UNITS, PAIR * (s % GROUP_UNITS)
-            term_tile = work.tile([P, PAIR], F32)
+            var_term[s] = []
             for i in range(PAIR):
-                scaled = work.tile([P, D], BF16)
-                nc.vector.tensor_scalar(
-                    out=scaled[:],
-                    in0=var_rows[g][:, first + i, :],
-                    scalar1=-LAMDA,
-                    scalar2=None,
-                    op0=ALU.mult,
-                    op1=ALU.add,
-                    accum_out=term_tile[:, i : i + 1],
-                )
-            var_term[s] = term_tile
+                term_tile = terms.tile([P, 1], F32)
+                if (PAIR * s + i) % SCALAR_SUM_EVERY == SCALAR_SUM_EVERY - 1:
+                    scaled_by_scalar = work.tile([P, D], BF16)
+                    nc.scalar.activation(
+                        out=scaled_by_scalar[:],
+                        in_=var_rows[g][:, first + i, :],
+                        func=ACT.Copy,
+                        scale=-LAMDA,
+                        accum_out=term_tile[:],
+                    )
+                else:
+                    scaled_by_vector = work.tile([P, D], BF16)
+                    nc.vector.tensor_scalar(
+                        out=scaled_by_vector[:],
+                        in0=var_rows[g][:, first + i, :],
+                        scalar1=-LAMDA,
+                        scalar2=None,
+                        op0=ALU.mult,
+                        op1=ALU.add,
+                        accum_out=term_tile[:],
+                    )
+                var_term[s].append(term_tile)
 
         def transposes(s):
             g, first = s // GROUP_UNITS, PAIR * (s % GROUP_UNITS)
@@ -232,7 +245,7 @@ def tile_probprotoseghead_t_e_kernel(
                 nc.vector.scalar_tensor_tensor(
                     out=out_rows[g][:, first + i, :],
                     in0=acc[s][:, i, :],
-                    scalar=var_term[s][:, i : i + 1],
+                    scalar=var_term[s][i][:],
                     in1=proto_term[:],
                     op0=ALU.add,
                     op1=ALU.add,

@@ -20,11 +20,13 @@ PROTOS = 256
 LAMDA = 1.0 / D
 PACK = 4
 PAIR = 2
-GROUP_TILES = 4
-GROUP_UNITS = GROUP_TILES // PAIR
+UNIT = PAIR * P
+GROUP_UNITS = 2
+GROUP_TILES = GROUP_UNITS * PAIR
 GROUPS = ROWS // (P * GROUP_TILES)
 UNITS = GROUPS * GROUP_UNITS
 LOADS_AHEAD = 5
+RUN = 2
 SCALAR_SUM_EVERY = 6
 
 FLOPS = 2 * 2 * ROWS * D * PROTOS
@@ -41,21 +43,28 @@ def tile_probprotoseghead_t_e_kernel(
     with ExitStack() as stack:
         const = stack.enter_context(tc.tile_pool(name="const", bufs=1))
         rows = stack.enter_context(tc.tile_pool(name="rows", bufs=LOADS_AHEAD + 1))
-        results = stack.enter_context(tc.tile_pool(name="results", bufs=3))
         work = stack.enter_context(tc.tile_pool(name="work", bufs=4))
         terms = stack.enter_context(tc.tile_pool(name="terms", bufs=4 * PAIR))
-        setup_psum = stack.enter_context(tc.psum_pool(name="setup_psum", bufs=1))
-        psum = stack.enter_context(tc.psum_pool(name="psum", bufs=2))
+        x_banks = stack.enter_context(tc.psum_pool(name="x_banks", bufs=RUN + 1))
+        var_banks = stack.enter_context(tc.psum_pool(name="var_banks", bufs=RUN + 1))
+        acc_banks = stack.enter_context(tc.psum_pool(name="acc_banks", bufs=RUN))
 
         ident = const.tile([P, P], F32)
         make_identity(nc, ident[:])
 
-        pv = const.tile([P, 2, D], BF16)
+        def transpose_rows(bank, i, row_tile, neighbours):
+            words = row_tile.bitcast(F32)
+            for u in range(2):
+                columns = words[:, u : D // 2 : 2] if neighbours else words[:, u * P : (u + 1) * P]
+                nc.tensor.transpose(
+                    out=bank[:, u, i * P : (i + 1) * P], in_=columns, identity=ident[:]
+                )
+
+        pv = const.tile([P, PAIR, D], BF16)
         nc.sync.dma_start(
             out=pv[:],
-            in_=proto_var.rearrange("c m d -> (c m) d").rearrange("(h p) d -> p h d", p=P),
+            in_=proto_var.rearrange("c m d -> (c m) d").rearrange("(i p) d -> p i d", p=P),
         )
-
         proto_codes = const.tile([P, PROTOS], U32, align_bytes=64)
         nc.sync.dma_start(
             out=proto_codes[:].bitcast(I32).rearrange("p (c m) -> p c m", m=PER_CLASS),
@@ -74,41 +83,35 @@ def tile_probprotoseghead_t_e_kernel(
                 in_=scale_words[:, 4 * quadrant : 4 * quadrant + 4, :].rearrange("c r w -> r c w"),
             )
 
-        pv_sum = const.tile([P, 2], F32)
+        pv_sum = const.tile([P, PAIR], F32)
         nc.vector.tensor_reduce(out=pv_sum[:], in_=pv[:], axis=mybir.AxisListType.X, op=ALU.add)
-        pv_term = const.tile([P, 2], F32)
+        pv_term = const.tile([P, PAIR], F32)
         nc.vector.tensor_scalar(
             out=pv_term[:], in0=pv_sum[:], scalar1=-LAMDA, scalar2=-2.0, op0=ALU.mult, op1=ALU.add
         )
-        spread = setup_psum.tile([P, 2, P], F32)
-        for h in range(2):
+        term_bank = acc_banks.tile([P, PROTOS], F32, tag="acc_bank")
+        for i in range(PAIR):
             nc.tensor.transpose(
-                out=spread[:, h, :],
-                in_=pv_term[:, h : h + 1].to_broadcast([P, P]),
+                out=term_bank[:, i * P : (i + 1) * P],
+                in_=pv_term[:, i : i + 1].to_broadcast([P, P]),
                 identity=ident[:],
             )
         proto_term = const.tile([P, PROTOS], F32)
-        nc.vector.tensor_copy(out=proto_term[:], in_=spread[:].rearrange("p h c -> p (h c)"))
+        nc.vector.tensor_copy(out=proto_term[:], in_=term_bank[:])
 
-        pv_t = setup_psum.tile([P, 2, 2, P], F32)
-        for h in range(2):
-            for u in range(2):
-                nc.tensor.transpose(
-                    out=pv_t[:, h, u, :],
-                    in_=pv[:, h, :].bitcast(F32)[:, u * P : (u + 1) * P],
-                    identity=ident[:],
-                )
-        pv_root = const.tile([P, 2, P, PACK], F32)
-        for h in range(2):
-            nc.scalar.activation(
-                out=pv_root[:, h].rearrange("p c (u e) -> p c u e", e=2),
-                in_=pv_t[:, h].bitcast(BF16).rearrange("p u (c e) -> p c u e", e=2),
-                func=ACT.Sqrt,
-            )
+        pv_bank = var_banks.tile([P, 2, PROTOS], F32, tag="var_bank")
+        for i in range(PAIR):
+            transpose_rows(pv_bank, i, pv[:, i, :], neighbours=False)
+        pv_root = const.tile([P, PROTOS, PACK], F32)
+        nc.scalar.activation(
+            out=pv_root[:].rearrange("p n (u e) -> p n u e", e=2),
+            in_=pv_bank[:].bitcast(BF16).rearrange("p u (n e) -> p n u e", e=2),
+            func=ACT.Sqrt,
+        )
         pv_grouped = const.tile([P, PROTOS * PACK], BF16, align_bytes=64)
         nc.vector.tensor_scalar(
             out=pv_grouped[:],
-            in0=pv_root[:].rearrange("p h c t -> p (h c t)"),
+            in0=pv_root[:].rearrange("p n t -> p (n t)"),
             scalar1=2.0 * LAMDA,
             scalar2=None,
             op0=ALU.mult,
@@ -121,14 +124,16 @@ def tile_probprotoseghead_t_e_kernel(
 
         x_rows = {}
         var_rows = {}
-        out_rows = {}
         var_term = {}
-        x_t = {}
-        var_t = {}
+        x_bank = {}
+        var_bank = {}
         grouped = {}
         codes = {}
         scales = {}
-        acc = {}
+        acc_bank = {}
+
+        def row_tile(group_rows, s, i):
+            return group_rows[s // GROUP_UNITS][:, PAIR * (s % GROUP_UNITS) + i, :]
 
         def load(g):
             x_tile = rows.tile([P, GROUP_TILES, D], BF16)
@@ -139,7 +144,6 @@ def tile_probprotoseghead_t_e_kernel(
             var_rows[g] = var_tile
 
         def sums(s):
-            g, first = s // GROUP_UNITS, PAIR * (s % GROUP_UNITS)
             var_term[s] = []
             for i in range(PAIR):
                 term_tile = terms.tile([P, 1], F32)
@@ -147,7 +151,7 @@ def tile_probprotoseghead_t_e_kernel(
                     scaled_by_scalar = work.tile([P, D], BF16)
                     nc.scalar.activation(
                         out=scaled_by_scalar[:],
-                        in_=var_rows[g][:, first + i, :],
+                        in_=row_tile(var_rows, s, i),
                         func=ACT.Copy,
                         scale=-LAMDA,
                         accum_out=term_tile[:],
@@ -156,7 +160,7 @@ def tile_probprotoseghead_t_e_kernel(
                     scaled_by_vector = work.tile([P, D], BF16)
                     nc.vector.tensor_scalar(
                         out=scaled_by_vector[:],
-                        in0=var_rows[g][:, first + i, :],
+                        in0=row_tile(var_rows, s, i),
                         scalar1=-LAMDA,
                         scalar2=None,
                         op0=ALU.mult,
@@ -166,58 +170,46 @@ def tile_probprotoseghead_t_e_kernel(
                 var_term[s].append(term_tile)
 
         def transposes(s):
-            g, first = s // GROUP_UNITS, PAIR * (s % GROUP_UNITS)
-            x_bank = psum.tile([P, PAIR, 2, P], F32)
-            var_bank = psum.tile([P, PAIR, 2, P], F32)
+            x_tile = x_banks.tile([P, 2, UNIT], F32, tag="x_bank")
+            var_tile = var_banks.tile([P, 2, UNIT], F32, tag="var_bank")
             for i in range(PAIR):
-                for u in range(2):
-                    nc.tensor.transpose(
-                        out=x_bank[:, i, u, :],
-                        in_=x_rows[g][:, first + i, :].bitcast(F32)[:, u : D // 2 : 2],
-                        identity=ident[:],
-                    )
+                transpose_rows(x_tile, i, row_tile(x_rows, s, i), neighbours=True)
             for i in range(PAIR):
-                for u in range(2):
-                    nc.tensor.transpose(
-                        out=var_bank[:, i, u, :],
-                        in_=var_rows[g][:, first + i, :].bitcast(F32)[:, u * P : (u + 1) * P],
-                        identity=ident[:],
-                    )
-            x_t[s] = x_bank
-            var_t[s] = var_bank
+                transpose_rows(var_tile, i, row_tile(var_rows, s, i), neighbours=False)
+            x_bank[s] = x_tile
+            var_bank[s] = var_tile
 
         def evacuate(s):
-            grouped_tile = work.tile([P, 2, PAIR, P, PACK], BF16, align_bytes=64)
+            grouped_tile = work.tile([P, 2, UNIT, PACK], BF16, align_bytes=64)
             nc.scalar.copy(
-                out=grouped_tile[:, 0].bitcast(F32), in_=x_t[s][:].rearrange("p i u n -> p i n u")
+                out=grouped_tile[:, 0].bitcast(F32), in_=x_bank[s][:].rearrange("p u n -> p n u")
             )
-            for i in range(PAIR):
-                nc.scalar.activation(
-                    out=grouped_tile[:, 1, i].rearrange("p n (u e) -> p n u e", e=2),
-                    in_=var_t[s][:, i].bitcast(BF16).rearrange("p u (n e) -> p n u e", e=2),
-                    func=ACT.Sqrt,
-                )
+            nc.scalar.activation(
+                out=grouped_tile[:, 1].rearrange("p n (u e) -> p n u e", e=2),
+                in_=var_bank[s][:].bitcast(BF16).rearrange("p u (n e) -> p n u e", e=2),
+                func=ACT.Sqrt,
+            )
             grouped[s] = grouped_tile
 
         def quantise(s):
-            codes_tile = work.tile([P, 2 * PAIR * P], U32, align_bytes=64)
-            scales_tile = work.tile([P, 2 * PAIR * P], U8, align_bytes=64)
+            codes_tile = work.tile([P, 2 * UNIT], U32, align_bytes=64)
+            scales_tile = work.tile([P, 2 * UNIT], U8, align_bytes=64)
             nc.vector.quantize_mx(
                 out=codes_tile[:].bitcast(FP8X4),
                 scales=scales_tile[:],
-                in_=grouped[s][:].rearrange("p k i n t -> p (k i n t)"),
+                in_=grouped[s][:].rearrange("p k n t -> p (k n t)"),
             )
             codes[s] = codes_tile
             scales[s] = scales_tile
 
         def multiply(s):
-            acc_bank = psum.tile([P, PAIR, PROTOS], F32)
+            acc_tile = acc_banks.tile([P, PAIR, PROTOS], F32, tag="acc_bank")
             for i in range(PAIR):
                 x_cols = slice(i * P, (i + 1) * P)
-                root_cols = slice((PAIR + i) * P, (PAIR + i + 1) * P)
+                root_cols = slice(UNIT + i * P, UNIT + (i + 1) * P)
                 for repeat in range(2):
                     nc.tensor.matmul_mx(
-                        out=acc_bank[:, i, :],
+                        out=acc_tile[:, i, :],
                         lhsT=codes[s][:, x_cols].bitcast(FP8X4),
                         lhsT_scale=scales[s][:, x_cols],
                         rhs=proto_codes[:].bitcast(FP8X4),
@@ -226,7 +218,7 @@ def tile_probprotoseghead_t_e_kernel(
                         stop=False,
                     )
                 nc.tensor.matmul_mx(
-                    out=acc_bank[:, i, :],
+                    out=acc_tile[:, i, :],
                     lhsT=codes[s][:, root_cols].bitcast(FP8X4),
                     lhsT_scale=scales[s][:, root_cols],
                     rhs=root_codes[:].bitcast(FP8X4),
@@ -234,38 +226,40 @@ def tile_probprotoseghead_t_e_kernel(
                     start=False,
                     stop=True,
                 )
-            acc[s] = acc_bank
+            acc_bank[s] = acc_tile
 
         def finish(s):
-            g, first = s // GROUP_UNITS, PAIR * (s % GROUP_UNITS)
-            if first == 0:
-                out_tile = results.tile([P, GROUP_TILES, PROTOS], F32)
-                out_rows[g] = out_tile
+            out_tile = work.tile([P, PAIR, PROTOS], F32)
             for i in range(PAIR):
                 nc.vector.scalar_tensor_tensor(
-                    out=out_rows[g][:, first + i, :],
-                    in0=acc[s][:, i, :],
+                    out=out_tile[:, i, :],
+                    in0=acc_bank[s][:, i, :],
                     scalar=var_term[s][i][:],
                     in1=proto_term[:],
                     op0=ALU.add,
                     op1=ALU.add,
                 )
-            if first + PAIR == GROUP_TILES:
-                nc.sync.dma_start(out=out_groups[g], in_=out_rows[g][:])
+            first = PAIR * (s % GROUP_UNITS)
+            nc.sync.dma_start(
+                out=out_groups[s // GROUP_UNITS][:, first : first + PAIR, :], in_=out_tile[:]
+            )
 
         with tc.manual_schedule():
             for g in range(LOADS_AHEAD):
                 load(g)
             for step in range(UNITS + 2):
+                if step % GROUP_UNITS == 0 and step // GROUP_UNITS + LOADS_AHEAD < GROUPS:
+                    load(step // GROUP_UNITS + LOADS_AHEAD)
+                if step % RUN == 0 and step < UNITS:
+                    for s in range(step, step + RUN):
+                        transposes(s)
                 if step < UNITS:
-                    if step % GROUP_UNITS == 0 and step // GROUP_UNITS + LOADS_AHEAD < GROUPS:
-                        load(step // GROUP_UNITS + LOADS_AHEAD)
-                    transposes(step)
                     evacuate(step)
-                if step >= 2:
-                    multiply(step - 2)
                 if 1 <= step <= UNITS:
                     quantise(step - 1)
+                if step % RUN == 0 and step >= RUN:
+                    for s in range(step - RUN, step):
+                        multiply(s)
                 if step >= 2:
                     finish(step - 2)
                 if step < UNITS:

@@ -26,7 +26,8 @@ GROUP_TILES = GROUP_UNITS * PAIR
 GROUPS = ROWS // (P * GROUP_TILES)
 UNITS = GROUPS * GROUP_UNITS
 LOADS_AHEAD = 5
-RUN = 2
+LAG = 2
+RUN = 1
 SCALAR_SUM_EVERY = 6
 
 FLOPS = 2 * 2 * ROWS * D * PROTOS
@@ -45,9 +46,9 @@ def tile_probprotoseghead_t_e_kernel(
         rows = stack.enter_context(tc.tile_pool(name="rows", bufs=LOADS_AHEAD + 1))
         work = stack.enter_context(tc.tile_pool(name="work", bufs=4))
         terms = stack.enter_context(tc.tile_pool(name="terms", bufs=4 * PAIR))
-        x_banks = stack.enter_context(tc.psum_pool(name="x_banks", bufs=RUN + 1))
-        var_banks = stack.enter_context(tc.psum_pool(name="var_banks", bufs=RUN + 1))
-        acc_banks = stack.enter_context(tc.psum_pool(name="acc_banks", bufs=RUN))
+        x_banks = stack.enter_context(tc.psum_pool(name="x_banks", bufs=3))
+        var_banks = stack.enter_context(tc.psum_pool(name="var_banks", bufs=3))
+        acc_banks = stack.enter_context(tc.psum_pool(name="acc_banks", bufs=2))
 
         ident = const.tile([P, P], F32)
         make_identity(nc, ident[:])
@@ -247,7 +248,7 @@ def tile_probprotoseghead_t_e_kernel(
         with tc.manual_schedule():
             for g in range(LOADS_AHEAD):
                 load(g)
-            for step in range(UNITS + 2):
+            for step in range(UNITS + LAG):
                 if step % GROUP_UNITS == 0 and step // GROUP_UNITS + LOADS_AHEAD < GROUPS:
                     load(step // GROUP_UNITS + LOADS_AHEAD)
                 if step % RUN == 0 and step < UNITS:
@@ -257,10 +258,10 @@ def tile_probprotoseghead_t_e_kernel(
                     evacuate(step)
                 if 1 <= step <= UNITS:
                     quantise(step - 1)
-                if step % RUN == 0 and step >= RUN:
-                    for s in range(step - RUN, step):
+                if step % RUN == 0 and step >= LAG:
+                    for s in range(step - LAG, step - LAG + RUN):
                         multiply(s)
-                if step >= 2:
-                    finish(step - 2)
+                if step >= LAG:
+                    finish(step - LAG)
                 if step < UNITS:
                     sums(step)

from contextlib import ExitStack

import concourse.mybir as mybir
from concourse.masks import make_identity

F32 = mybir.dt.float32
BF16 = mybir.dt.bfloat16
I32 = mybir.dt.int32
U32 = mybir.dt.uint32
U8 = mybir.dt.uint8
FP8X4 = mybir.dt.float8_e4m3fn_x4
ALU = mybir.AluOpType
ACT = mybir.ActivationFunctionType

P = 128
ROWS = 12288
D = 512
PER_CLASS = 16
PROTOS = 256
LAMDA = 1.0 / D
PACK = 4
PAIR = 2
UNIT = PAIR * P
GROUP_UNITS = 2
GROUP_TILES = GROUP_UNITS * PAIR
GROUPS = ROWS // (P * GROUP_TILES)
UNITS = GROUPS * GROUP_UNITS
LOADS_AHEAD = 5
LAG = 2
RUN = 1
SCALAR_SUM_EVERY = 6

FLOPS = 2 * 2 * ROWS * D * PROTOS


def tile_probprotoseghead_t_e_kernel(
    tc, x, x_var, prototypes_words, prototypes_scales, proto_var, out
):
    nc = tc.nc
    x_groups = x.rearrange("(g p t) d -> g p t d", p=P, t=GROUP_TILES)
    var_groups = x_var.rearrange("(g p t) d -> g p t d", p=P, t=GROUP_TILES)
    out_groups = out.rearrange("(g p t) c m -> g p t (c m)", p=P, t=GROUP_TILES)

    with ExitStack() as stack:
        const = stack.enter_context(tc.tile_pool(name="const", bufs=1))
        rows = stack.enter_context(tc.tile_pool(name="rows", bufs=LOADS_AHEAD + 1))
        work = stack.enter_context(tc.tile_pool(name="work", bufs=4))
        terms = stack.enter_context(tc.tile_pool(name="terms", bufs=4 * PAIR))
        x_banks = stack.enter_context(tc.psum_pool(name="x_banks", bufs=3))
        var_banks = stack.enter_context(tc.psum_pool(name="var_banks", bufs=3))
        acc_banks = stack.enter_context(tc.psum_pool(name="acc_banks", bufs=2))

        ident = const.tile([P, P], F32)
        make_identity(nc, ident[:])

        def transpose_rows(bank, i, row_tile, neighbours):
            words = row_tile.bitcast(F32)
            for u in range(2):
                columns = words[:, u : D // 2 : 2] if neighbours else words[:, u * P : (u + 1) * P]
                nc.tensor.transpose(
                    out=bank[:, u, i * P : (i + 1) * P], in_=columns, identity=ident[:]
                )

        pv = const.tile([P, PAIR, D], BF16)
        nc.sync.dma_start(
            out=pv[:],
            in_=proto_var.rearrange("c m d -> (c m) d").rearrange("(i p) d -> p i d", p=P),
        )
        proto_codes = const.tile([P, PROTOS], U32, align_bytes=64)
        nc.sync.dma_start(
            out=proto_codes[:].bitcast(I32).rearrange("p (c m) -> p c m", m=PER_CLASS),
            in_=prototypes_words.rearrange("c p m t -> c p (m t)")
            .bitcast(I32)
            .rearrange("c p m -> p c m"),
        )
        proto_scales = const.tile([P, PROTOS], U8, align_bytes=64)
        nc.vector.memset(proto_scales[:].bitcast(I32), 0)
        scale_words = prototypes_scales.bitcast(I32)
        for quadrant in range(4):
            nc.sync.dma_start(
                out=proto_scales[32 * quadrant : 32 * quadrant + 4, :]
                .bitcast(I32)
                .rearrange("r (c w) -> r c w", w=PER_CLASS // 4),
                in_=scale_words[:, 4 * quadrant : 4 * quadrant + 4, :].rearrange("c r w -> r c w"),
            )

        pv_sum = const.tile([P, PAIR], F32)
        nc.vector.tensor_reduce(out=pv_sum[:], in_=pv[:], axis=mybir.AxisListType.X, op=ALU.add)
        pv_term = const.tile([P, PAIR], F32)
        nc.vector.tensor_scalar(
            out=pv_term[:], in0=pv_sum[:], scalar1=-LAMDA, scalar2=-2.0, op0=ALU.mult, op1=ALU.add
        )
        term_bank = acc_banks.tile([P, PROTOS], F32, tag="acc_bank")
        for i in range(PAIR):
            nc.tensor.transpose(
                out=term_bank[:, i * P : (i + 1) * P],
                in_=pv_term[:, i : i + 1].to_broadcast([P, P]),
                identity=ident[:],
            )
        proto_term = const.tile([P, PROTOS], F32)
        nc.vector.tensor_copy(out=proto_term[:], in_=term_bank[:])

        pv_bank = var_banks.tile([P, 2, PROTOS], F32, tag="var_bank")
        for i in range(PAIR):
            transpose_rows(pv_bank, i, pv[:, i, :], neighbours=False)
        pv_root = const.tile([P, PROTOS, PACK], F32)
        nc.scalar.activation(
            out=pv_root[:].rearrange("p n (u e) -> p n u e", e=2),
            in_=pv_bank[:].bitcast(BF16).rearrange("p u (n e) -> p n u e", e=2),
            func=ACT.Sqrt,
        )
        pv_grouped = const.tile([P, PROTOS * PACK], BF16, align_bytes=64)
        nc.vector.tensor_scalar(
            out=pv_grouped[:],
            in0=pv_root[:].rearrange("p n t -> p (n t)"),
            scalar1=2.0 * LAMDA,
            scalar2=None,
            op0=ALU.mult,
        )
        root_codes = const.tile([P, PROTOS], U32, align_bytes=64)
        root_scales = const.tile([P, PROTOS], U8, align_bytes=64)
        nc.vector.quantize_mx(
            out=root_codes[:].bitcast(FP8X4), scales=root_scales[:], in_=pv_grouped[:]
        )

        x_rows = {}
        var_rows = {}
        var_term = {}
        x_bank = {}
        var_bank = {}
        grouped = {}
        codes = {}
        scales = {}
        acc_bank = {}

        def row_tile(group_rows, s, i):
            return group_rows[s // GROUP_UNITS][:, PAIR * (s % GROUP_UNITS) + i, :]

        def load(g):
            x_tile = rows.tile([P, GROUP_TILES, D], BF16)
            nc.sync.dma_start(out=x_tile[:], in_=x_groups[g])
            var_tile = rows.tile([P, GROUP_TILES, D], BF16)
            nc.sync.dma_start(out=var_tile[:], in_=var_groups[g])
            x_rows[g] = x_tile
            var_rows[g] = var_tile

        def sums(s):
            var_term[s] = []
            for i in range(PAIR):
                term_tile = terms.tile([P, 1], F32)
                if (PAIR * s + i) % SCALAR_SUM_EVERY == SCALAR_SUM_EVERY - 1:
                    scaled_by_scalar = work.tile([P, D], BF16)
                    nc.scalar.activation(
                        out=scaled_by_scalar[:],
                        in_=row_tile(var_rows, s, i),
                        func=ACT.Copy,
                        scale=-LAMDA,
                        accum_out=term_tile[:],
                    )
                else:
                    scaled_by_vector = work.tile([P, D], BF16)
                    nc.vector.tensor_scalar(
                        out=scaled_by_vector[:],
                        in0=row_tile(var_rows, s, i),
                        scalar1=-LAMDA,
                        scalar2=None,
                        op0=ALU.mult,
                        op1=ALU.add,
                        accum_out=term_tile[:],
                    )
                var_term[s].append(term_tile)

        def transposes(s):
            x_tile = x_banks.tile([P, 2, UNIT], F32, tag="x_bank")
            var_tile = var_banks.tile([P, 2, UNIT], F32, tag="var_bank")
            for i in range(PAIR):
                transpose_rows(x_tile, i, row_tile(x_rows, s, i), neighbours=True)
            for i in range(PAIR):
                transpose_rows(var_tile, i, row_tile(var_rows, s, i), neighbours=False)
            x_bank[s] = x_tile
            var_bank[s] = var_tile

        def evacuate(s):
            grouped_tile = work.tile([P, 2, UNIT, PACK], BF16, align_bytes=64)
            nc.scalar.copy(
                out=grouped_tile[:, 0].bitcast(F32), in_=x_bank[s][:].rearrange("p u n -> p n u")
            )
            nc.scalar.activation(
                out=grouped_tile[:, 1].rearrange("p n (u e) -> p n u e", e=2),
                in_=var_bank[s][:].bitcast(BF16).rearrange("p u (n e) -> p n u e", e=2),
                func=ACT.Sqrt,
            )
            grouped[s] = grouped_tile

        def quantise(s):
            codes_tile = work.tile([P, 2 * UNIT], U32, align_bytes=64)
            scales_tile = work.tile([P, 2 * UNIT], U8, align_bytes=64)
            nc.vector.quantize_mx(
                out=codes_tile[:].bitcast(FP8X4),
                scales=scales_tile[:],
                in_=grouped[s][:].rearrange("p k n t -> p (k n t)"),
            )
            codes[s] = codes_tile
            scales[s] = scales_tile

        def multiply(s):
            acc_tile = acc_banks.tile([P, PAIR, PROTOS], F32, tag="acc_bank")
            for i in range(PAIR):
                x_cols = slice(i * P, (i + 1) * P)
                root_cols = slice(UNIT + i * P, UNIT + (i + 1) * P)
                for repeat in range(2):
                    nc.tensor.matmul_mx(
                        out=acc_tile[:, i, :],
                        lhsT=codes[s][:, x_cols].bitcast(FP8X4),
                        lhsT_scale=scales[s][:, x_cols],
                        rhs=proto_codes[:].bitcast(FP8X4),
                        rhs_scale=proto_scales[:],
                        start=(repeat == 0),
                        stop=False,
                    )
                nc.tensor.matmul_mx(
                    out=acc_tile[:, i, :],
                    lhsT=codes[s][:, root_cols].bitcast(FP8X4),
                    lhsT_scale=scales[s][:, root_cols],
                    rhs=root_codes[:].bitcast(FP8X4),
                    rhs_scale=root_scales[:],
                    start=False,
                    stop=True,
                )
            acc_bank[s] = acc_tile

        def finish(s):
            out_tile = work.tile([P, PAIR, PROTOS], F32)
            for i in range(PAIR):
                nc.vector.scalar_tensor_tensor(
                    out=out_tile[:, i, :],
                    in0=acc_bank[s][:, i, :],
                    scalar=var_term[s][i][:],
                    in1=proto_term[:],
                    op0=ALU.add,
                    op1=ALU.add,
                )
            first = PAIR * (s % GROUP_UNITS)
            nc.sync.dma_start(
                out=out_groups[s // GROUP_UNITS][:, first : first + PAIR, :], in_=out_tile[:]
            )

        with tc.manual_schedule():
            for g in range(LOADS_AHEAD):
                load(g)
            for step in range(UNITS + LAG):
                if step % GROUP_UNITS == 0 and step // GROUP_UNITS + LOADS_AHEAD < GROUPS:
                    load(step // GROUP_UNITS + LOADS_AHEAD)
                if step % RUN == 0 and step < UNITS:
                    for s in range(step, step + RUN):
                        transposes(s)
                if step < UNITS:
                    evacuate(step)
                if 1 <= step <= UNITS:
                    quantise(step - 1)
                if step % RUN == 0 and step >= LAG:
                    for s in range(step - LAG, step - LAG + RUN):
                        multiply(s)
                if step >= LAG:
                    finish(step - LAG)
                if step < UNITS:
                    sums(step)
